import numpy as np
import ml_dtypes


def mxq(x, axis, fmt="e4m3"):
    dtype, down = {"e4m3": (ml_dtypes.float8_e4m3fn, 7), "e5m2": (ml_dtypes.float8_e5m2, 14)}[fmt]
    v = np.moveaxis(np.asarray(x, np.float32).astype(ml_dtypes.bfloat16).astype(np.float64), axis, -1)
    blocks = v.reshape(v.shape[:-1] + (-1, 32))
    amax = np.abs(blocks).max(-1, keepdims=True)
    byte = np.maximum(np.where(amax > 0, np.frexp(amax)[1] - 1 + 127, 0) - down, 1)
    scale = np.exp2(byte - 127.0)
    codes = (blocks / scale).astype(np.float32).astype(dtype).astype(np.float64)
    return np.moveaxis((codes * scale).reshape(v.shape), -1, axis)


WIDE = False


def mx_kscale(k):
    if not WIDE:
        return np.ones(k)
    levels = np.array([10, -10, 5, -5, 0])
    a = np.random.permutation(np.resize(levels, k // 512 * 4)).reshape(k // 512, 4)
    idx = np.arange(k)
    return np.exp2(a[idx // 512, idx % 128 // 32])


BF16 = ml_dtypes.bfloat16


def bf(x):
    return np.asarray(x, np.float32).astype(BF16)


def f64(x):
    return np.asarray(x).astype(np.float64)


N, NB, D = 16384, 512, 128

INV_SQRT_2PI = 1.0 / np.sqrt(2.0 * np.pi)


def phi(t):
    return INV_SQRT_2PI * np.exp(-0.5 * t * t)


def setup_inputs():
    a = np.log2(mx_kscale(NB))
    u = np.exp2(np.round(1.2 * (a - a.min())))
    g = np.where(u > 1.0, np.where(u == u.max(), 0.25, 0.1), 1.0)
    q_mu = 0.5 + 0.2 * np.random.standard_normal(N)
    q_sigma_sq = 0.01 + 0.1 * np.random.random(N)
    theta = np.stack([q_mu / q_sigma_sq, -0.5 / q_sigma_sq], axis=1)
    basis_mu = np.linspace(0.0, 1.0, NB) + 0.01 * np.random.standard_normal(NB)
    basis_sigma = 0.05 * (1.0 + 0.1 * np.random.standard_normal(NB)) * u
    Bv = np.random.standard_normal((NB, D)) * 0.64 / np.sqrt(NB) * (u * g)[:, None]
    return {"theta": bf(theta), "basis_mu": bf(basis_mu), "basis_sigma": bf(basis_sigma), "Bv": bf(Bv)}


def reference(theta, basis_mu, basis_sigma, Bv):
    theta, basis_mu, basis_sigma, Bv = f64(theta), f64(basis_mu), f64(basis_sigma), f64(Bv)
    sigma_sq = -0.5 / theta[:, 1]
    mu = theta[:, 0] * sigma_sq
    s = np.sqrt(basis_sigma[None, :] ** 2 + sigma_sq[:, None])
    r = phi((mu[:, None] - basis_mu[None, :]) / s) / s
    context = mxq(r, 1, "e4m3") @ mxq(Bv, 0, "e4m3")
    return context

@@ -1,0 +1,207 @@
+from contextlib import ExitStack
+import math
+
+import concourse.mybir as mybir
+from concourse.masks import make_identity
+
+F32 = mybir.dt.float32
+BF16 = mybir.dt.bfloat16
+U32 = mybir.dt.uint32
+U8 = mybir.dt.uint8
+FP8X4 = mybir.dt.float8_e4m3fn_x4
+ACT = mybir.ActivationFunctionType
+ALU = mybir.AluOpType
+
+N, NB, D = 16384, 512, 128
+FLOPS = 2 * N * NB * D
+P = 128
+NG = 32
+CH = 8
+TWO_PI = 2.0 * math.pi
+HEAD = 16
+
+QG = [0] * NG
+QV = [1, 2] * (NG // 2)
+
+
+def tile_longtermattention_t_kernel(tc, theta, basis_mu, basis_sigma, Bv, out):
+    nc = tc.nc
+    with ExitStack() as ctx:
+        const = ctx.enter_context(tc.tile_pool(name="const", bufs=1))
+        gpool = ctx.enter_context(tc.tile_pool(name="gpool", bufs=CH))
+        zpool = ctx.enter_context(tc.tile_pool(name="zpool", bufs=CH))
+        rpool = ctx.enter_context(tc.tile_pool(name="rpool", bufs=3))
+        qpool = ctx.enter_context(tc.tile_pool(name="qpool", bufs=3))
+        opool = ctx.enter_context(tc.tile_pool(name="opool", bufs=3))
+        ps_s = ctx.enter_context(tc.psum_pool(name="ps_s", bufs=3))
+        ps_m = ctx.enter_context(tc.psum_pool(name="ps_m", bufs=3))
+        ps_o = ctx.enter_context(tc.psum_pool(name="ps_o", bufs=2))
+        ctx.enter_context(tc.manual_schedule())
+
+        th = const.tile([P, P, 2], BF16)
+        nc.sync.dma_start(out=th[:], in_=theta.rearrange("(p c) k -> p c k", c=P))
+        bs_raw = const.tile([P, 4], BF16)
+        nc.sync.dma_start(out=bs_raw[:], in_=basis_sigma.rearrange("(p t) -> p t", t=4))
+        bm_raw = const.tile([P, 4], BF16)
+        nc.sync.dma_start(out=bm_raw[:], in_=basis_mu.rearrange("(p t) -> p t", t=4))
+        bv_raw = const.tile([P, 4, D], BF16)
+        nc.sync.dma_start(out=bv_raw[:], in_=Bv.rearrange("(p t) d -> p t d", t=4))
+
+        ident = const.tile([P, P], F32)
+        make_identity(nc, ident[:])
+
+        parts = []
+        for lo, hi, nm in ((0, HEAD, "a"), (HEAD, P, "b")):
+            w = hi - lo
+            rec = const.tile([P, w], F32, name="rec" + nm)
+            sig = const.tile([P, w], F32, name="sig" + nm)
+            mu = const.tile([P, w], F32, name="mu" + nm)
+            parts.append((lo, hi, rec, sig, mu))
+
+        def head_part(k):
+            lo, hi, rec, sig, mu = parts[k]
+            nc.vector.reciprocal(out=rec[:], in_=th[:, lo:hi, 1])
+            nc.vector.tensor_scalar_mul(out=sig[:], in0=rec[:], scalar1=-0.5)
+            nc.vector.tensor_tensor(out=mu[:], in0=sig[:], in1=th[:, lo:hi, 0], op=ALU.mult)
+
+        head_part(0)
+        b2 = const.tile([P, 4], F32)
+        nc.vector.scalar_tensor_tensor(out=b2[:], in0=bs_raw[:], scalar=TWO_PI, in1=bs_raw[:],
+                                       op0=ALU.mult, op1=ALU.mult)
+        bm = const.tile([P, 4], F32)
+        nc.vector.tensor_copy(out=bm[:], in_=bm_raw[:])
+        head_part(1)
+
+        bvg = const.tile([P, D, 4], BF16, align_bytes=64)
+        nc.vector.tensor_copy(out=bvg[:], in_=bv_raw[:].rearrange("p t d -> p d t"))
+        bvc = const.tile([P, D], U32, align_bytes=64)
+        bvs = const.tile([P, D], U8, align_bytes=64)
+
+        def col(which, c):
+            k = 0 if c < HEAD else 1
+            lo = parts[k][0]
+            return parts[k][which][:, c - lo:c - lo + 1].to_broadcast([P, P])
+
+        sb, mb, gt, zt, rt, ct, st, ot, osb = {}, {}, {}, {}, {}, {}, {}, {}, {}
+
+        def bcast(i, which, pool, store, nm):
+            if i >= NG:
+                return
+            t = pool.tile([P, 512], F32, name=nm)
+            for q in range(4):
+                nc.tensor.transpose(t[:, P * q:P * (q + 1)], col(which, 4 * i + q), ident[:])
+            store[i] = t
+
+        def do_r(i):
+            g = gpool.tile([P, 4, 512], F32, name="g")
+            for t in range(4):
+                nc.scalar.activation(out=g[:, t, :], in_=sb[i][:], func=ACT.Abs_reciprocal_sqrt,
+                                     bias=b2[:, t:t + 1], scale=TWO_PI)
+            gt[i] = g
+
+        def do_z(i):
+            z = zpool.tile([P, 4, 512], F32, name="z")
+            for t in range(4):
+                nc.vector.scalar_tensor_tensor(out=z[:, t, :], in0=mb[i][:], scalar=bm[:, t:t + 1],
+                                               in1=gt[i][:, t, :], op0=ALU.subtract, op1=ALU.mult)
+            zt[i] = z
+
+        def sq_view(i, a, b):
+            return zt[i][:, a:b, :].rearrange("p t n -> p (t n)")
+
+        def do_qg(i):
+            if QG[i] > 0:
+                v = sq_view(i, 0, QG[i])
+                nc.gpsimd.tensor_tensor(out=v, in0=v, in1=v, op=ALU.mult)
+
+        def do_qv(i):
+            if QV[i] > 0:
+                v = sq_view(i, QG[i], QG[i] + QV[i])
+                nc.vector.tensor_tensor(out=v, in0=v, in1=v, op=ALU.mult)
+
+        def do_qa(i):
+            if QG[i] + QV[i] < 4:
+                v = sq_view(i, QG[i] + QV[i], 4)
+                nc.scalar.activation(out=v, in_=v, func=ACT.Square)
+
+        def do_e(i):
+            v = sq_view(i, 0, 4)
+            nc.scalar.activation(out=v, in_=v, func=ACT.Exp, scale=-math.pi)
+
+        def do_p(i):
+            r = rpool.tile([P, 512, 4], BF16, name="r", align_bytes=64)
+            nc.vector.tensor_tensor(
+                out=r[:].rearrange("p (c i) t -> p c t i", i=4),
+                in0=zt[i][:].rearrange("p t (c i) -> p c t i", i=4),
+                in1=gt[i][:].rearrange("p t (c i) -> p c t i", i=4),
+                op=ALU.mult)
+            rt[i] = r
+
+        def do_quant(i):
+            codes = qpool.tile([P, 512], U32, name="codes", align_bytes=64)
+            scl = qpool.tile([P, 512], U8, name="scl", align_bytes=64)
+            nc.vector.quantize_mx(out=codes[:].bitcast(FP8X4), scales=scl[:],
+                                  in_=rt[i][:].rearrange("p n t -> p (n t)"))
+            acc = ps_o.tile([P, 512], F32, name="acc")
+            for q in range(4):
+                cs = slice(P * q, P * (q + 1))
+                nc.tensor.matmul_mx(out=acc[:, cs], lhsT=codes[:, cs].bitcast(FP8X4),
+                                    lhsT_scale=scl[:, cs], rhs=bvc[:].bitcast(FP8X4),
+                                    rhs_scale=bvs[:], start=True, stop=True)
+            ot[i] = acc
+
+        out_v = out.rearrange("(p c) d -> p c d", c=P)
+
+        def do_evac(i):
+            s, q = divmod(i, 4)
+            if q == 0:
+                osb[s] = opool.tile([P, 16, D], F32, name="osb")
+            nc.vector.tensor_copy(out=osb[s][:, 4 * q:4 * q + 4, :].rearrange("p c d -> p (c d)"),
+                                  in_=ot[i][:])
+            if q == 3:
+                nc.sync.dma_start(out=out_v[:, 16 * s:16 * s + 16, :], in_=osb[s][:])
+
+        slot = [0]
+        deferred = {}
+
+        def defer(s, item):
+            deferred[s] = deferred.get(s, []) + [item]
+
+        def after_slot():
+            for kind, i in deferred.get(slot[0], []):
+                if kind == 0:
+                    do_quant(i)
+                else:
+                    do_evac(i)
+            slot[0] = slot[0] + 1
+
+        for i in range(3):
+            bcast(i, 3, ps_s, sb, "sb")
+            bcast(i, 4, ps_m, mb, "mb")
+
+        first = True
+        for a in range(0, NG, CH):
+            grp = list(range(a, min(a + CH, NG)))
+            for i in grp:
+                do_r(i)
+                bcast(i + 3, 3, ps_s, sb, "sb")
+                do_z(i)
+                bcast(i + 3, 4, ps_m, mb, "mb")
+                do_qg(i)
+                if i > a:
+                    do_qv(i - 1)
+                after_slot()
+                if first:
+                    nc.vector.quantize_mx(out=bvc[:].bitcast(FP8X4), scales=bvs[:],
+                                          in_=bvg[:].rearrange("p d t -> p (d t)"))
+                    first = False
+            do_qv(grp[-1])
+            for i in grp:
+                do_qa(i)
+                do_e(i)
+                do_p(i)
+                defer(slot[0] + 1, (0, i))
+                defer(slot[0] + 2, (1, i))
+                after_slot()
+        for k in range(3):
+            after_slot()

@@ -16,12 +16,14 @@ N, NB, D = 16384, 512, 128
 FLOPS = 2 * N * NB * D
 P = 128
 NG = 32
-CH = 8
+SIZES = (11, 11, 10)
+CH = 11
 TWO_PI = 2.0 * math.pi
 HEAD = 16
 
-QG = [0] * NG
-QV = [1, 2] * (NG // 2)
+QG = [2] * NG
+QV = [0] * NG
+EV_ACT = 29
 
 
 def tile_longtermattention_t_kernel(tc, theta, basis_mu, basis_sigma, Bv, out):
@@ -156,9 +158,14 @@ def tile_longtermattention_t_kernel(tc, theta, basis_mu, basis_sigma, Bv, out):
             s, q = divmod(i, 4)
             if q == 0:
                 osb[s] = opool.tile([P, 16, D], F32, name="osb")
-            nc.vector.tensor_copy(out=osb[s][:, 4 * q:4 * q + 4, :].rearrange("p c d -> p (c d)"),
-                                  in_=ot[i][:])
-            if q == 3:
+            dst = osb[s][:, 4 * q:4 * q + 4, :].rearrange("p c d -> p (c d)")
+            if i >= EV_ACT:
+                nc.scalar.copy(out=dst, in_=ot[i][:])
+            else:
+                nc.vector.tensor_copy(out=dst, in_=ot[i][:])
+            if s == NG // 4 - 1:
+                nc.sync.dma_start(out=out_v[:, 4 * i:4 * i + 4, :], in_=osb[s][:, 4 * q:4 * q + 4, :])
+            elif q == 3:
                 nc.sync.dma_start(out=out_v[:, 16 * s:16 * s + 16, :], in_=osb[s][:])
 
         slot = [0]
@@ -180,8 +187,10 @@ def tile_longtermattention_t_kernel(tc, theta, basis_mu, basis_sigma, Bv, out):
             bcast(i, 4, ps_m, mb, "mb")
 
         first = True
-        for a in range(0, NG, CH):
-            grp = list(range(a, min(a + CH, NG)))
+        starts = [sum(SIZES[:k]) for k in range(len(SIZES))]
+        for a, size in zip(starts, SIZES):
+            grp = list(range(a, a + size))
+            after_slot()
             for i in grp:
                 do_r(i)
                 bcast(i + 3, 3, ps_s, sb, "sb")

@@ -21,9 +21,9 @@ CH = 11
 TWO_PI = 2.0 * math.pi
 HEAD = 16
 
-QG = [2] * NG
-QV = [0] * NG
-EV_ACT = 29
+QA = [0] * NG
+POOL_PIECES = 2
+EV_DVE = ()
 
 
 def tile_longtermattention_t_kernel(tc, theta, basis_mu, basis_sigma, Bv, out):
@@ -35,8 +35,8 @@ def tile_longtermattention_t_kernel(tc, theta, basis_mu, basis_sigma, Bv, out):
         rpool = ctx.enter_context(tc.tile_pool(name="rpool", bufs=3))
         qpool = ctx.enter_context(tc.tile_pool(name="qpool", bufs=3))
         opool = ctx.enter_context(tc.tile_pool(name="opool", bufs=3))
-        ps_s = ctx.enter_context(tc.psum_pool(name="ps_s", bufs=3))
-        ps_m = ctx.enter_context(tc.psum_pool(name="ps_m", bufs=3))
+        ps_s = ctx.enter_context(tc.psum_pool(name="ps_s", bufs=2))
+        ps_t = ctx.enter_context(tc.psum_pool(name="ps_t", bufs=4))
         ps_o = ctx.enter_context(tc.psum_pool(name="ps_o", bufs=2))
         ctx.enter_context(tc.manual_schedule())
 
@@ -66,12 +66,34 @@ def tile_longtermattention_t_kernel(tc, theta, basis_mu, basis_sigma, Bv, out):
             nc.vector.tensor_scalar_mul(out=sig[:], in0=rec[:], scalar1=-0.5)
             nc.vector.tensor_tensor(out=mu[:], in0=sig[:], in1=th[:, lo:hi, 0], op=ALU.mult)
 
+        def col(which, c):
+            k = 0 if c < HEAD else 1
+            lo = parts[k][0]
+            return parts[k][which][:, c - lo:c - lo + 1]
+
+        sb, gt, gp, zt, ep, rt, ot, osb = {}, {}, {}, {}, {}, {}, {}, {}
+
+        def do_s(i):
+            if i >= NG:
+                return
+            t = ps_s.tile([P, 512], F32, name="sb")
+            for q in range(4):
+                nc.tensor.transpose(t[:, P * q:P * (q + 1)], col(3, 4 * i + q).to_broadcast([P, P]), ident[:])
+            sb[i] = t
+
         head_part(0)
+        do_s(0)
+        do_s(1)
         b2 = const.tile([P, 4], F32)
         nc.vector.scalar_tensor_tensor(out=b2[:], in0=bs_raw[:], scalar=TWO_PI, in1=bs_raw[:],
                                        op0=ALU.mult, op1=ALU.mult)
         bm = const.tile([P, 4], F32)
         nc.vector.tensor_copy(out=bm[:], in_=bm_raw[:])
+        bmp = ps_t.tile([P, 512], F32, name="tp")
+        for t in range(4):
+            nc.tensor.transpose(bmp[:, P * t:P * (t + 1)], bm[:, t:t + 1].to_broadcast([P, P]), ident[:])
+        bmc = const.tile([P, 512], F32)
+        nc.vector.tensor_copy(out=bmc[:], in_=bmp[:])
         head_part(1)
 
         bvg = const.tile([P, D, 4], BF16, align_bytes=64)
@@ -79,65 +101,59 @@ def tile_longtermattention_t_kernel(tc, theta, basis_mu, basis_sigma, Bv, out):
         bvc = const.tile([P, D], U32, align_bytes=64)
         bvs = const.tile([P, D], U8, align_bytes=64)
 
-        def col(which, c):
-            k = 0 if c < HEAD else 1
-            lo = parts[k][0]
-            return parts[k][which][:, c - lo:c - lo + 1].to_broadcast([P, P])
-
-        sb, mb, gt, zt, rt, ct, st, ot, osb = {}, {}, {}, {}, {}, {}, {}, {}, {}
-
-        def bcast(i, which, pool, store, nm):
-            if i >= NG:
-                return
-            t = pool.tile([P, 512], F32, name=nm)
-            for q in range(4):
-                nc.tensor.transpose(t[:, P * q:P * (q + 1)], col(which, 4 * i + q), ident[:])
-            store[i] = t
-
-        def do_r(i):
+        def do_g(i):
             g = gpool.tile([P, 4, 512], F32, name="g")
             for t in range(4):
                 nc.scalar.activation(out=g[:, t, :], in_=sb[i][:], func=ACT.Abs_reciprocal_sqrt,
                                      bias=b2[:, t:t + 1], scale=TWO_PI)
             gt[i] = g
 
-        def do_z(i):
-            z = zpool.tile([P, 4, 512], F32, name="z")
+        def do_t(i, q):
+            t_ps = ps_t.tile([P, 512], F32, name="tp")
             for t in range(4):
-                nc.vector.scalar_tensor_tensor(out=z[:, t, :], in0=mb[i][:], scalar=bm[:, t:t + 1],
-                                               in1=gt[i][:, t, :], op0=ALU.subtract, op1=ALU.mult)
-            zt[i] = z
+                nc.tensor.transpose(t_ps[:, P * t:P * (t + 1)], gt[i][:, t, P * q:P * (q + 1)], ident[:])
+            gp[(i, q)] = t_ps
+
+        def do_z(i, q):
+            if q == 0:
+                zt[i] = zpool.tile([P, 4, 512], F32, name="z")
+            nc.vector.scalar_tensor_tensor(out=zt[i][:, q, :], in0=bmc[:], scalar=col(4, 4 * i + q),
+                                           in1=gp[(i, q)][:], op0=ALU.subtract, op1=ALU.mult)
 
         def sq_view(i, a, b):
-            return zt[i][:, a:b, :].rearrange("p t n -> p (t n)")
+            return zt[i][:, a:b, :].rearrange("p q n -> p (q n)")
 
         def do_qg(i):
-            if QG[i] > 0:
-                v = sq_view(i, 0, QG[i])
+            n_pool = 4 - QA[i]
+            step = max(1, n_pool // POOL_PIECES)
+            for a in range(0, n_pool, step):
+                v = sq_view(i, a, min(n_pool, a + step))
                 nc.gpsimd.tensor_tensor(out=v, in0=v, in1=v, op=ALU.mult)
 
-        def do_qv(i):
-            if QV[i] > 0:
-                v = sq_view(i, QG[i], QG[i] + QV[i])
-                nc.vector.tensor_tensor(out=v, in0=v, in1=v, op=ALU.mult)
-
         def do_qa(i):
-            if QG[i] + QV[i] < 4:
-                v = sq_view(i, QG[i] + QV[i], 4)
+            if QA[i] > 0:
+                v = sq_view(i, 4 - QA[i], 4)
                 nc.scalar.activation(out=v, in_=v, func=ACT.Square)
 
         def do_e(i):
             v = sq_view(i, 0, 4)
             nc.scalar.activation(out=v, in_=v, func=ACT.Exp, scale=-math.pi)
 
-        def do_p(i):
-            r = rpool.tile([P, 512, 4], BF16, name="r", align_bytes=64)
+        def do_et(i, q):
+            t_ps = ps_t.tile([P, 512], F32, name="tp")
+            for t in range(4):
+                nc.tensor.transpose(t_ps[:, P * t:P * (t + 1)], zt[i][:, q, P * t:P * (t + 1)], ident[:])
+            ep[(i, q)] = t_ps
+
+        def do_p(i, q):
+            if q == 0:
+                rt[i] = rpool.tile([P, 512, 4], BF16, name="r", align_bytes=64)
+            cs = slice(P * q, P * (q + 1))
             nc.vector.tensor_tensor(
-                out=r[:].rearrange("p (c i) t -> p c t i", i=4),
-                in0=zt[i][:].rearrange("p t (c i) -> p c t i", i=4),
-                in1=gt[i][:].rearrange("p t (c i) -> p c t i", i=4),
+                out=rt[i][:, cs, :].rearrange("p (c i) t -> p c t i", i=4),
+                in0=ep[(i, q)][:].rearrange("p (t c i) -> p c t i", t=4, i=4),
+                in1=gt[i][:, :, cs].rearrange("p t (c i) -> p c t i", i=4),
                 op=ALU.mult)
-            rt[i] = r
 
         def do_quant(i):
             codes = qpool.tile([P, 512], U32, name="codes", align_bytes=64)
@@ -159,10 +175,10 @@ def tile_longtermattention_t_kernel(tc, theta, basis_mu, basis_sigma, Bv, out):
             if q == 0:
                 osb[s] = opool.tile([P, 16, D], F32, name="osb")
             dst = osb[s][:, 4 * q:4 * q + 4, :].rearrange("p c d -> p (c d)")
-            if i >= EV_ACT:
-                nc.scalar.copy(out=dst, in_=ot[i][:])
-            else:
+            if i in EV_DVE:
                 nc.vector.tensor_copy(out=dst, in_=ot[i][:])
+            else:
+                nc.scalar.copy(out=dst, in_=ot[i][:])
             if s == NG // 4 - 1:
                 nc.sync.dma_start(out=out_v[:, 4 * i:4 * i + 4, :], in_=osb[s][:, 4 * q:4 * q + 4, :])
             elif q == 3:
@@ -182,33 +198,34 @@ def tile_longtermattention_t_kernel(tc, theta, basis_mu, basis_sigma, Bv, out):
                     do_evac(i)
             slot[0] = slot[0] + 1
 
-        for i in range(3):
-            bcast(i, 3, ps_s, sb, "sb")
-            bcast(i, 4, ps_m, mb, "mb")
-
         first = True
         starts = [sum(SIZES[:k]) for k in range(len(SIZES))]
         for a, size in zip(starts, SIZES):
-            grp = list(range(a, a + size))
-            after_slot()
-            for i in grp:
-                do_r(i)
-                bcast(i + 3, 3, ps_s, sb, "sb")
-                do_z(i)
-                bcast(i + 3, 4, ps_m, mb, "mb")
+            b = a + size
+            for i in range(a, b):
+                do_g(i)
+                for q in range(4):
+                    do_t(i, q)
+                    do_z(i, q)
+                do_s(i + 2)
                 do_qg(i)
-                if i > a:
-                    do_qv(i - 1)
                 after_slot()
                 if first:
                     nc.vector.quantize_mx(out=bvc[:].bitcast(FP8X4), scales=bvs[:],
                                           in_=bvg[:].rearrange("p d t -> p (d t)"))
                     first = False
-            do_qv(grp[-1])
-            for i in grp:
-                do_qa(i)
-                do_e(i)
-                do_p(i)
+            do_qa(a)
+            do_e(a)
+            for q in range(4):
+                do_et(a, q)
+            for i in range(a, b):
+                if i + 1 < b:
+                    do_qa(i + 1)
+                    do_e(i + 1)
+                for q in range(4):
+                    do_p(i, q)
+                    if i + 1 < b:
+                        do_et(i + 1, q)
                 defer(slot[0] + 1, (0, i))
                 defer(slot[0] + 2, (1, i))
                 after_slot()

@@ -21,9 +21,12 @@ CH = 11
 TWO_PI = 2.0 * math.pi
 HEAD = 16
 
-QA = [0] * NG
+QA = [{0: 4, 1: 2}.get(b - 1 - i, 0) for b, n in ((11, 11), (22, 11), (32, 10)) for i in range(b - n, b)]
+QSTART = 7
+QRATE = 2
 POOL_PIECES = 2
 EV_DVE = ()
+LEAD = 3
 
 
 def tile_longtermattention_t_kernel(tc, theta, basis_mu, basis_sigma, Bv, out):
@@ -32,7 +35,6 @@ def tile_longtermattention_t_kernel(tc, theta, basis_mu, basis_sigma, Bv, out):
         const = ctx.enter_context(tc.tile_pool(name="const", bufs=1))
         gpool = ctx.enter_context(tc.tile_pool(name="gpool", bufs=CH))
         zpool = ctx.enter_context(tc.tile_pool(name="zpool", bufs=CH))
-        rpool = ctx.enter_context(tc.tile_pool(name="rpool", bufs=3))
         qpool = ctx.enter_context(tc.tile_pool(name="qpool", bufs=3))
         opool = ctx.enter_context(tc.tile_pool(name="opool", bufs=3))
         ps_s = ctx.enter_context(tc.psum_pool(name="ps_s", bufs=2))
@@ -116,7 +118,7 @@ def tile_longtermattention_t_kernel(tc, theta, basis_mu, basis_sigma, Bv, out):
 
         def do_z(i, q):
             if q == 0:
-                zt[i] = zpool.tile([P, 4, 512], F32, name="z")
+                zt[i] = zpool.tile([P, 4, 512], F32, name="z", align_bytes=64)
             nc.vector.scalar_tensor_tensor(out=zt[i][:, q, :], in0=bmc[:], scalar=col(4, 4 * i + q),
                                            in1=gp[(i, q)][:], op0=ALU.subtract, op1=ALU.mult)
 
@@ -135,9 +137,11 @@ def tile_longtermattention_t_kernel(tc, theta, basis_mu, basis_sigma, Bv, out):
                 v = sq_view(i, 4 - QA[i], 4)
                 nc.scalar.activation(out=v, in_=v, func=ACT.Square)
 
-        def do_e(i):
-            v = sq_view(i, 0, 4)
-            nc.scalar.activation(out=v, in_=v, func=ACT.Exp, scale=-math.pi)
+        def do_e(i, pieces=1):
+            w = 4 // pieces
+            for k in range(pieces):
+                v = sq_view(i, w * k, w * (k + 1))
+                nc.scalar.activation(out=v, in_=v, func=ACT.Exp, scale=-math.pi)
 
         def do_et(i, q):
             t_ps = ps_t.tile([P, 512], F32, name="tp")
@@ -147,7 +151,8 @@ def tile_longtermattention_t_kernel(tc, theta, basis_mu, basis_sigma, Bv, out):
 
         def do_p(i, q):
             if q == 0:
-                rt[i] = rpool.tile([P, 512, 4], BF16, name="r", align_bytes=64)
+                rt[i] = zt[i][:].rearrange("p q n -> p (q n)").bitcast(BF16)[:, 0:2048].rearrange(
+                    "p (n t) -> p n t", t=4)
             cs = slice(P * q, P * (q + 1))
             nc.vector.tensor_tensor(
                 out=rt[i][:, cs, :].rearrange("p (c i) t -> p c t i", i=4),
@@ -159,7 +164,7 @@ def tile_longtermattention_t_kernel(tc, theta, basis_mu, basis_sigma, Bv, out):
             codes = qpool.tile([P, 512], U32, name="codes", align_bytes=64)
             scl = qpool.tile([P, 512], U8, name="scl", align_bytes=64)
             nc.vector.quantize_mx(out=codes[:].bitcast(FP8X4), scales=scl[:],
-                                  in_=rt[i][:].rearrange("p n t -> p (n t)"))
+                                  in_=rt[i].rearrange("p n t -> p (n t)"))
             acc = ps_o.tile([P, 512], F32, name="acc")
             for q in range(4):
                 cs = slice(P * q, P * (q + 1))
@@ -184,19 +189,21 @@ def tile_longtermattention_t_kernel(tc, theta, basis_mu, basis_sigma, Bv, out):
             elif q == 3:
                 nc.sync.dma_start(out=out_v[:, 16 * s:16 * s + 16, :], in_=osb[s][:])
 
-        slot = [0]
-        deferred = {}
+        done = [0, 0, 0]
 
-        def defer(s, item):
-            deferred[s] = deferred.get(s, []) + [item]
+        def emit_quant(n):
+            for k in range(min(n, done[0] - done[1])):
+                do_quant(done[1])
+                done[1] = done[1] + 1
+                if done[1] - done[2] > 1:
+                    do_evac(done[2])
+                    done[2] = done[2] + 1
 
-        def after_slot():
-            for kind, i in deferred.get(slot[0], []):
-                if kind == 0:
-                    do_quant(i)
-                else:
-                    do_evac(i)
-            slot[0] = slot[0] + 1
+        def flush():
+            emit_quant(NG)
+            for i in range(done[2], done[1]):
+                do_evac(i)
+            done[2] = done[1]
 
         first = True
         starts = [sum(SIZES[:k]) for k in range(len(SIZES))]
@@ -204,30 +211,31 @@ def tile_longtermattention_t_kernel(tc, theta, basis_mu, basis_sigma, Bv, out):
             b = a + size
             for i in range(a, b):
                 do_g(i)
+                if i == a:
+                    flush()
                 for q in range(4):
                     do_t(i, q)
                     do_z(i, q)
                 do_s(i + 2)
                 do_qg(i)
-                after_slot()
                 if first:
                     nc.vector.quantize_mx(out=bvc[:].bitcast(FP8X4), scales=bvs[:],
                                           in_=bvg[:].rearrange("p d t -> p (d t)"))
                     first = False
-            do_qa(a)
-            do_e(a)
+            for i in range(a, min(b, a + LEAD)):
+                do_qa(i)
+                do_e(i, 4 if i == a else 1)
             for q in range(4):
                 do_et(a, q)
             for i in range(a, b):
-                if i + 1 < b:
-                    do_qa(i + 1)
-                    do_e(i + 1)
+                if i + LEAD < b:
+                    do_qa(i + LEAD)
+                    do_e(i + LEAD)
+                if i - a >= QSTART:
+                    emit_quant(QRATE)
                 for q in range(4):
                     do_p(i, q)
                     if i + 1 < b:
                         do_et(i + 1, q)
-                defer(slot[0] + 1, (0, i))
-                defer(slot[0] + 2, (1, i))
-                after_slot()
-        for k in range(3):
-            after_slot()
+                done[0] = i + 1
+        flush()

@@ -21,12 +21,14 @@ CH = 11
 TWO_PI = 2.0 * math.pi
 HEAD = 16
 
-QA = [{0: 4, 1: 2}.get(b - 1 - i, 0) for b, n in ((11, 11), (22, 11), (32, 10)) for i in range(b - n, b)]
-QSTART = 7
-QRATE = 2
+N_ACT = 1
+K_ACT = 7
 POOL_PIECES = 2
-EV_DVE = ()
+EV_DVE_EVERY = 99
 LEAD = 3
+QSTART = 99
+QRATE = 2
+PRE_G = 2
 
 
 def tile_longtermattention_t_kernel(tc, theta, basis_mu, basis_sigma, Bv, out):
@@ -102,6 +104,8 @@ def tile_longtermattention_t_kernel(tc, theta, basis_mu, basis_sigma, Bv, out):
         nc.vector.tensor_copy(out=bvg[:], in_=bv_raw[:].rearrange("p t d -> p d t"))
         bvc = const.tile([P, D], U32, align_bytes=64)
         bvs = const.tile([P, D], U8, align_bytes=64)
+        nc.vector.quantize_mx(out=bvc[:].bitcast(FP8X4), scales=bvs[:],
+                              in_=bvg[:].rearrange("p d t -> p (d t)"))
 
         def do_g(i):
             g = gpool.tile([P, 4, 512], F32, name="g")
@@ -126,16 +130,14 @@ def tile_longtermattention_t_kernel(tc, theta, basis_mu, basis_sigma, Bv, out):
             return zt[i][:, a:b, :].rearrange("p q n -> p (q n)")
 
         def do_qg(i):
-            n_pool = 4 - QA[i]
-            step = max(1, n_pool // POOL_PIECES)
-            for a in range(0, n_pool, step):
-                v = sq_view(i, a, min(n_pool, a + step))
+            step = 4 // POOL_PIECES
+            for a in range(0, 4, step):
+                v = sq_view(i, a, a + step)
                 nc.gpsimd.tensor_tensor(out=v, in0=v, in1=v, op=ALU.mult)
 
         def do_qa(i):
-            if QA[i] > 0:
-                v = sq_view(i, 4 - QA[i], 4)
-                nc.scalar.activation(out=v, in_=v, func=ACT.Square)
+            v = sq_view(i, 0, 4)
+            nc.scalar.activation(out=v, in_=v, func=ACT.Square)
 
         def do_e(i, pieces=1):
             w = 4 // pieces
@@ -180,7 +182,7 @@ def tile_longtermattention_t_kernel(tc, theta, basis_mu, basis_sigma, Bv, out):
             if q == 0:
                 osb[s] = opool.tile([P, 16, D], F32, name="osb")
             dst = osb[s][:, 4 * q:4 * q + 4, :].rearrange("p c d -> p (c d)")
-            if i in EV_DVE:
+            if i % EV_DVE_EVERY == EV_DVE_EVERY - 1:
                 nc.vector.tensor_copy(out=dst, in_=ot[i][:])
             else:
                 nc.scalar.copy(out=dst, in_=ot[i][:])
@@ -205,37 +207,64 @@ def tile_longtermattention_t_kernel(tc, theta, basis_mu, basis_sigma, Bv, out):
                 do_evac(i)
             done[2] = done[1]
 
-        first = True
+        made = [0]
+        spread = [2]
+
+        def next_g(limit):
+            if made[0] < min(limit, spread[0]):
+                do_g(made[0])
+                made[0] = made[0] + 1
+
+        def next_s():
+            if spread[0] < min(NG, made[0] + 2):
+                do_s(spread[0])
+                spread[0] = spread[0] + 1
+
         starts = [sum(SIZES[:k]) for k in range(len(SIZES))]
         for a, size in zip(starts, SIZES):
             b = a + size
             for i in range(a, b):
-                do_g(i)
+                next_g(min(b, i + 2))
+                next_g(min(b, i + 2))
                 if i == a:
+                    for q in range(4):
+                        do_t(i, q)
                     flush()
-                for q in range(4):
-                    do_t(i, q)
-                    do_z(i, q)
-                do_s(i + 2)
-                do_qg(i)
-                if first:
-                    nc.vector.quantize_mx(out=bvc[:].bitcast(FP8X4), scales=bvs[:],
-                                          in_=bvg[:].rearrange("p d t -> p (d t)"))
-                    first = False
-            for i in range(a, min(b, a + LEAD)):
-                do_qa(i)
-                do_e(i, 4 if i == a else 1)
+                    for q in range(4):
+                        do_z(i, q)
+                else:
+                    for q in range(4):
+                        do_t(i, q)
+                        do_z(i, q)
+                next_s()
+                next_s()
+                if i < b - N_ACT:
+                    do_qg(i)
+            k_act = min(K_ACT, size - N_ACT)
+            order = list(range(a, a + k_act)) + list(range(b - N_ACT, b)) + list(range(a + k_act, b - N_ACT))
+
+            def exp_of(k):
+                if k < size:
+                    if order[k] >= b - N_ACT:
+                        do_qa(order[k])
+                    do_e(order[k], 4 if k == 0 else 1)
+                else:
+                    next_g(min(NG, b + PRE_G))
+
+            for k in range(LEAD):
+                exp_of(k)
             for q in range(4):
-                do_et(a, q)
-            for i in range(a, b):
-                if i + LEAD < b:
-                    do_qa(i + LEAD)
-                    do_e(i + LEAD)
-                if i - a >= QSTART:
+                do_et(order[0], q)
+            for k in range(size):
+                exp_of(k + LEAD)
+                if k >= QSTART:
                     emit_quant(QRATE)
                 for q in range(4):
-                    do_p(i, q)
-                    if i + 1 < b:
-                        do_et(i + 1, q)
-                done[0] = i + 1
+                    do_p(order[k], q)
+                    if k + 1 < size:
+                        do_et(order[k + 1], q)
+                if k + 1 >= k_act + N_ACT:
+                    done[0] = order[k] + 1 if k + 1 < size else b
+                elif k < k_act:
+                    done[0] = order[k] + 1
         flush()

@@ -21,13 +21,12 @@ CH = 11
 TWO_PI = 2.0 * math.pi
 HEAD = 16
 
-N_ACT = 1
+A_TILES = 3
 K_ACT = 7
-POOL_PIECES = 2
+FINE = 0
+POOL_PIECES = 1
 EV_DVE_EVERY = 99
 LEAD = 3
-QSTART = 99
-QRATE = 2
 PRE_G = 2
 
 
@@ -129,21 +128,18 @@ def tile_longtermattention_t_kernel(tc, theta, basis_mu, basis_sigma, Bv, out):
         def sq_view(i, a, b):
             return zt[i][:, a:b, :].rearrange("p q n -> p (q n)")
 
-        def do_qg(i):
-            step = 4 // POOL_PIECES
-            for a in range(0, 4, step):
-                v = sq_view(i, a, a + step)
+        def do_qg(i, lo=0, step=4 // POOL_PIECES):
+            for a in range(lo, 4, step):
+                v = sq_view(i, a, min(4, a + step))
                 nc.gpsimd.tensor_tensor(out=v, in0=v, in1=v, op=ALU.mult)
 
-        def do_qa(i):
-            v = sq_view(i, 0, 4)
+        def do_qa(i, hi):
+            v = sq_view(i, 0, hi)
             nc.scalar.activation(out=v, in_=v, func=ACT.Square)
 
-        def do_e(i, pieces=1):
-            w = 4 // pieces
-            for k in range(pieces):
-                v = sq_view(i, w * k, w * (k + 1))
-                nc.scalar.activation(out=v, in_=v, func=ACT.Exp, scale=-math.pi)
+        def do_e(i, lo, hi):
+            v = sq_view(i, lo, hi)
+            nc.scalar.activation(out=v, in_=v, func=ACT.Exp, scale=-math.pi)
 
         def do_et(i, q):
             t_ps = ps_t.tile([P, 512], F32, name="tp")
@@ -238,33 +234,40 @@ def tile_longtermattention_t_kernel(tc, theta, basis_mu, basis_sigma, Bv, out):
                         do_z(i, q)
                 next_s()
                 next_s()
-                if i < b - N_ACT:
+                if i < b - 1:
                     do_qg(i)
-            k_act = min(K_ACT, size - N_ACT)
-            order = list(range(a, a + k_act)) + list(range(b - N_ACT, b)) + list(range(a + k_act, b - N_ACT))
-
-            def exp_of(k):
-                if k < size:
-                    if order[k] >= b - N_ACT:
-                        do_qa(order[k])
-                    do_e(order[k], 4 if k == 0 else 1)
                 else:
+                    do_qg(i, A_TILES, 1)
+            k_act = min(K_ACT, size - 1)
+            runs = [(a, q, q + 1, False) for q in range(4)]
+            runs += [(i, 0, 4, False) for i in range(a + 1, a + k_act)]
+            if A_TILES > 0:
+                runs += [(b - 1, 0, A_TILES, True)]
+            runs += [(i, 0, 4, False) for i in range(a + k_act, b - 1 - FINE)]
+            runs += [(i, q, q + 1, False) for i in range(b - 1 - FINE, b - 1) for q in range(4)]
+            runs += [(b - 1, q, q + 1, False) for q in range(A_TILES, 4)]
+            units = [(i, q) for i, lo, hi, sq in runs for q in range(lo, hi)]
+            state = [0, 0]
+
+            def scalar_ahead(upto):
+                while state[1] < upto and state[0] < len(runs):
+                    i, lo, hi, sq = runs[state[0]]
+                    if sq:
+                        do_qa(i, hi)
+                    do_e(i, lo, hi)
+                    state[0] = state[0] + 1
+                    state[1] = state[1] + hi - lo
+                if state[0] == len(runs) and upto > len(units):
                     next_g(min(NG, b + PRE_G))
 
-            for k in range(LEAD):
-                exp_of(k)
-            for q in range(4):
-                do_et(order[0], q)
-            for k in range(size):
-                exp_of(k + LEAD)
-                if k >= QSTART:
-                    emit_quant(QRATE)
-                for q in range(4):
-                    do_p(order[k], q)
-                    if k + 1 < size:
-                        do_et(order[k + 1], q)
-                if k + 1 >= k_act + N_ACT:
-                    done[0] = order[k] + 1 if k + 1 < size else b
-                elif k < k_act:
-                    done[0] = order[k] + 1
+            scalar_ahead(4 * LEAD)
+            for u in units[0:4]:
+                do_et(u[0], u[1])
+            for k in range(len(units)):
+                if k % 4 == 0:
+                    scalar_ahead(k + 4 + 4 * LEAD)
+                do_p(units[k][0], units[k][1])
+                if k + 4 < len(units):
+                    do_et(units[k + 4][0], units[k + 4][1])
+            done[0] = b
         flush()

@@ -27,6 +27,7 @@ FINE = 0
 POOL_PIECES = 1
 EV_DVE_EVERY = 99
 LEAD = 3
+EV_LAG = 1
 PRE_G = 2
 
 
@@ -38,9 +39,8 @@ def tile_longtermattention_t_kernel(tc, theta, basis_mu, basis_sigma, Bv, out):
         zpool = ctx.enter_context(tc.tile_pool(name="zpool", bufs=CH))
         qpool = ctx.enter_context(tc.tile_pool(name="qpool", bufs=3))
         opool = ctx.enter_context(tc.tile_pool(name="opool", bufs=3))
-        ps_s = ctx.enter_context(tc.psum_pool(name="ps_s", bufs=2))
         ps_t = ctx.enter_context(tc.psum_pool(name="ps_t", bufs=4))
-        ps_o = ctx.enter_context(tc.psum_pool(name="ps_o", bufs=2))
+        ps_o = ctx.enter_context(tc.psum_pool(name="ps_o", bufs=4))
         ctx.enter_context(tc.manual_schedule())
 
         th = const.tile([P, P, 2], BF16)
@@ -79,7 +79,7 @@ def tile_longtermattention_t_kernel(tc, theta, basis_mu, basis_sigma, Bv, out):
         def do_s(i):
             if i >= NG:
                 return
-            t = ps_s.tile([P, 512], F32, name="sb")
+            t = ps_o.tile([P, 512], F32, name="acc")
             for q in range(4):
                 nc.tensor.transpose(t[:, P * q:P * (q + 1)], col(3, 4 * i + q).to_broadcast([P, P]), ident[:])
             sb[i] = t
@@ -193,7 +193,7 @@ def tile_longtermattention_t_kernel(tc, theta, basis_mu, basis_sigma, Bv, out):
             for k in range(min(n, done[0] - done[1])):
                 do_quant(done[1])
                 done[1] = done[1] + 1
-                if done[1] - done[2] > 1:
+                if done[1] - done[2] > EV_LAG:
                     do_evac(done[2])
                     done[2] = done[2] + 1
 

@@ -234,7 +234,9 @@ def tile_longtermattention_t_kernel(tc, theta, basis_mu, basis_sigma, Bv, out):
                         do_z(i, q)
                 next_s()
                 next_s()
-                if i < b - 1:
+                if i == a:
+                    do_qg(i, 0, 1)
+                elif i < b - 1:
                     do_qg(i)
                 else:
                     do_qg(i, A_TILES, 1)

@@ -16,18 +16,23 @@ N, NB, D = 16384, 512, 128
 FLOPS = 2 * N * NB * D
 P = 128
 NG = 32
-SIZES = (11, 11, 10)
-CH = 11
+SIZES = (10, 10, 12)
+BUFS = 12
+LOOK = 2
 TWO_PI = 2.0 * math.pi
+FIRST_SB = 8
+OB = 2
 HEAD = 16
 
-A_TILES = 3
+A_TILES = 2
 K_ACT = 7
 FINE = 0
 POOL_PIECES = 1
 EV_DVE_EVERY = 99
 LEAD = 3
 EV_LAG = 1
+TAIL_FROM = 9
+FL_G = 6
 PRE_G = 2
 
 
@@ -35,10 +40,11 @@ def tile_longtermattention_t_kernel(tc, theta, basis_mu, basis_sigma, Bv, out):
     nc = tc.nc
     with ExitStack() as ctx:
         const = ctx.enter_context(tc.tile_pool(name="const", bufs=1))
-        gpool = ctx.enter_context(tc.tile_pool(name="gpool", bufs=CH))
-        zpool = ctx.enter_context(tc.tile_pool(name="zpool", bufs=CH))
-        qpool = ctx.enter_context(tc.tile_pool(name="qpool", bufs=3))
-        opool = ctx.enter_context(tc.tile_pool(name="opool", bufs=3))
+        gpool = ctx.enter_context(tc.tile_pool(name="gpool", bufs=BUFS))
+        zpool = ctx.enter_context(tc.tile_pool(name="zpool", bufs=BUFS))
+        qpool = ctx.enter_context(tc.tile_pool(name="qpool", bufs=4))
+        spool = ctx.enter_context(tc.tile_pool(name="spool", bufs=3))
+        opool = ctx.enter_context(tc.tile_pool(name="opool", bufs=4))
         ps_t = ctx.enter_context(tc.psum_pool(name="ps_t", bufs=4))
         ps_o = ctx.enter_context(tc.psum_pool(name="ps_o", bufs=4))
         ctx.enter_context(tc.manual_schedule())
@@ -59,30 +65,41 @@ def tile_longtermattention_t_kernel(tc, theta, basis_mu, basis_sigma, Bv, out):
         for lo, hi, nm in ((0, HEAD, "a"), (HEAD, P, "b")):
             w = hi - lo
             rec = const.tile([P, w], F32, name="rec" + nm)
-            sig = const.tile([P, w], F32, name="sig" + nm)
             mu = const.tile([P, w], F32, name="mu" + nm)
-            parts.append((lo, hi, rec, sig, mu))
+            parts.append((lo, hi, rec, mu))
+        sig = const.tile([P, P], F32)
 
         def head_part(k):
-            lo, hi, rec, sig, mu = parts[k]
+            lo, hi, rec, mu = parts[k]
             nc.vector.reciprocal(out=rec[:], in_=th[:, lo:hi, 1])
-            nc.vector.tensor_scalar_mul(out=sig[:], in0=rec[:], scalar1=-0.5)
-            nc.vector.tensor_tensor(out=mu[:], in0=sig[:], in1=th[:, lo:hi, 0], op=ALU.mult)
+            nc.vector.tensor_scalar_mul(out=sig[:, lo:hi], in0=rec[:], scalar1=-0.5)
+            nc.vector.tensor_tensor(out=mu[:], in0=sig[:, lo:hi], in1=th[:, lo:hi, 0], op=ALU.mult)
 
-        def col(which, c):
-            k = 0 if c < HEAD else 1
-            lo = parts[k][0]
-            return parts[k][which][:, c - lo:c - lo + 1]
+        def mu_col(c):
+            lo, hi, rec, mu = parts[0 if c < HEAD else 1]
+            return mu[:, c - lo:c - lo + 1]
 
         sb, gt, gp, zt, ep, rt, ot, osb = {}, {}, {}, {}, {}, {}, {}, {}
 
         def do_s(i):
-            if i >= NG:
-                return
             t = ps_o.tile([P, 512], F32, name="acc")
             for q in range(4):
-                nc.tensor.transpose(t[:, P * q:P * (q + 1)], col(3, 4 * i + q).to_broadcast([P, P]), ident[:])
-            sb[i] = t
+                nc.tensor.transpose(t[:, P * q:P * (q + 1)], sig[:, 4 * i + q:4 * i + q + 1].to_broadcast([P, P]), ident[:])
+            sb[i] = t[:]
+
+        def store_sigma():
+            t = ps_o.tile([P, 512], F32, name="acc")
+            nc.tensor.transpose(t[:, 0:P], sig[:], ident[:])
+            sgt = const.tile([P, P], F32)
+            nc.vector.tensor_copy(out=sgt[:], in_=t[:, 0:P])
+            nc.sync.dma_start(out=out[N - P:N, :], in_=sgt[:])
+
+        def load_sigma(k):
+            t = spool.tile([P, 1024], F32, name="sgb")
+            lo = N - P + 8 * k
+            nc.sync.dma_start(out=t[:], in_=out[lo:lo + 8, :].rearrange("c m -> (c m)").partition_broadcast(P))
+            for j in range(2):
+                sb[2 * k + j] = t[:, 512 * j:512 * (j + 1)]
 
         head_part(0)
         do_s(0)
@@ -97,20 +114,22 @@ def tile_longtermattention_t_kernel(tc, theta, basis_mu, basis_sigma, Bv, out):
             nc.tensor.transpose(bmp[:, P * t:P * (t + 1)], bm[:, t:t + 1].to_broadcast([P, P]), ident[:])
         bmc = const.tile([P, 512], F32)
         nc.vector.tensor_copy(out=bmc[:], in_=bmp[:])
-        head_part(1)
 
         bvg = const.tile([P, D, 4], BF16, align_bytes=64)
-        nc.vector.tensor_copy(out=bvg[:], in_=bv_raw[:].rearrange("p t d -> p d t"))
         bvc = const.tile([P, D], U32, align_bytes=64)
         bvs = const.tile([P, D], U8, align_bytes=64)
-        nc.vector.quantize_mx(out=bvc[:].bitcast(FP8X4), scales=bvs[:],
-                              in_=bvg[:].rearrange("p d t -> p (d t)"))
+
+        def do_bv():
+            nc.vector.tensor_copy(out=bvg[:], in_=bv_raw[:].rearrange("p t d -> p d t"))
+            nc.vector.quantize_mx(out=bvc[:].bitcast(FP8X4), scales=bvs[:],
+                                  in_=bvg[:].rearrange("p d t -> p (d t)"))
 
         def do_g(i):
             g = gpool.tile([P, 4, 512], F32, name="g")
-            for t in range(4):
-                nc.scalar.activation(out=g[:, t, :], in_=sb[i][:], func=ACT.Abs_reciprocal_sqrt,
-                                     bias=b2[:, t:t + 1], scale=TWO_PI)
+            for cs in [slice(c, c + (128 if i == 0 else 512)) for c in range(0, 512, 128 if i == 0 else 512)]:
+                for t in range(4):
+                    nc.scalar.activation(out=g[:, t, cs], in_=sb[i][:, cs], func=ACT.Abs_reciprocal_sqrt,
+                                         bias=b2[:, t:t + 1], scale=TWO_PI)
             gt[i] = g
 
         def do_t(i, q):
@@ -122,7 +141,7 @@ def tile_longtermattention_t_kernel(tc, theta, basis_mu, basis_sigma, Bv, out):
         def do_z(i, q):
             if q == 0:
                 zt[i] = zpool.tile([P, 4, 512], F32, name="z", align_bytes=64)
-            nc.vector.scalar_tensor_tensor(out=zt[i][:, q, :], in0=bmc[:], scalar=col(4, 4 * i + q),
+            nc.vector.scalar_tensor_tensor(out=zt[i][:, q, :], in0=bmc[:], scalar=mu_col(4 * i + q),
                                            in1=gp[(i, q)][:], op0=ALU.subtract, op1=ALU.mult)
 
         def sq_view(i, a, b):
@@ -174,31 +193,35 @@ def tile_longtermattention_t_kernel(tc, theta, basis_mu, basis_sigma, Bv, out):
         out_v = out.rearrange("(p c) d -> p c d", c=P)
 
         def do_evac(i):
-            s, q = divmod(i, 4)
+            s, q = divmod(i, OB)
             if q == 0:
-                osb[s] = opool.tile([P, 16, D], F32, name="osb")
+                osb[s] = opool.tile([P, 4 * OB, D], F32, name="osb")
             dst = osb[s][:, 4 * q:4 * q + 4, :].rearrange("p c d -> p (c d)")
             if i % EV_DVE_EVERY == EV_DVE_EVERY - 1:
                 nc.vector.tensor_copy(out=dst, in_=ot[i][:])
             else:
                 nc.scalar.copy(out=dst, in_=ot[i][:])
-            if s == NG // 4 - 1:
+            if s == NG // OB - 1:
                 nc.sync.dma_start(out=out_v[:, 4 * i:4 * i + 4, :], in_=osb[s][:, 4 * q:4 * q + 4, :])
-            elif q == 3:
-                nc.sync.dma_start(out=out_v[:, 16 * s:16 * s + 16, :], in_=osb[s][:])
+            elif q == OB - 1:
+                nc.sync.dma_start(out=out_v[:, 4 * OB * s:4 * OB * (s + 1), :], in_=osb[s][:])
 
         done = [0, 0, 0]
 
-        def emit_quant(n):
+        def emit_quant(n, more=False):
+            if done[1] == 0 and done[0] > 0:
+                do_bv()
             for k in range(min(n, done[0] - done[1])):
+                if more and k == FL_G:
+                    next_g(NG)
                 do_quant(done[1])
                 done[1] = done[1] + 1
                 if done[1] - done[2] > EV_LAG:
                     do_evac(done[2])
                     done[2] = done[2] + 1
 
-        def flush():
-            emit_quant(NG)
+        def flush(more=False):
+            emit_quant(NG, more)
             for i in range(done[2], done[1]):
                 do_evac(i)
             done[2] = done[1]
@@ -207,60 +230,66 @@ def tile_longtermattention_t_kernel(tc, theta, basis_mu, basis_sigma, Bv, out):
         spread = [2]
 
         def next_g(limit):
-            if made[0] < min(limit, spread[0]):
+            if made[0] < limit:
                 do_g(made[0])
                 made[0] = made[0] + 1
+                if made[0] % 2 == 0 and FIRST_SB < made[0] + 4 < NG:
+                    load_sigma(made[0] // 2 + 2)
 
         def next_s():
-            if spread[0] < min(NG, made[0] + 2):
+            if spread[0] < min(FIRST_SB, made[0] + 2):
                 do_s(spread[0])
                 spread[0] = spread[0] + 1
 
-        starts = [sum(SIZES[:k]) for k in range(len(SIZES))]
-        for a, size in zip(starts, SIZES):
+        ga = 0
+        for ph, size in enumerate(SIZES):
+            a = sum(SIZES[:ph])
             b = a + size
-            for i in range(a, b):
-                next_g(min(b, i + 2))
-                next_g(min(b, i + 2))
-                if i == a:
+            gb = min(NG, b + LOOK)
+            last = b == NG
+            for i in range(ga, gb):
+                next_g(min(gb, i + 2))
+                if i == 0:
+                    next_g(min(gb, i + 2))
+                if i == 1:
+                    store_sigma()
+                    load_sigma(FIRST_SB // 2)
+                if i == ga:
                     for q in range(4):
                         do_t(i, q)
-                    flush()
+                    flush(i > 0)
                     for q in range(4):
                         do_z(i, q)
                 else:
                     for q in range(4):
                         do_t(i, q)
                         do_z(i, q)
+                if i == 0:
+                    head_part(1)
                 next_s()
                 next_s()
-                if i == a:
+                if i == ga:
                     do_qg(i, 0, 1)
-                elif i < b - 1:
+                elif i < gb - 1:
                     do_qg(i)
-                else:
+                elif A_TILES < 4:
                     do_qg(i, A_TILES, 1)
-            k_act = min(K_ACT, size - 1)
-            runs = [(a, q, q + 1, False) for q in range(4)]
-            runs += [(i, 0, 4, False) for i in range(a + 1, a + k_act)]
-            if A_TILES > 0:
-                runs += [(b - 1, 0, A_TILES, True)]
-            runs += [(i, 0, 4, False) for i in range(a + k_act, b - 1 - FINE)]
-            runs += [(i, q, q + 1, False) for i in range(b - 1 - FINE, b - 1) for q in range(4)]
-            runs += [(b - 1, q, q + 1, False) for q in range(A_TILES, 4)]
-            units = [(i, q) for i, lo, hi, sq in runs for q in range(lo, hi)]
+            runs = [(a, q, q + 1) for q in range(4)]
+            runs += [(i, 0, 4) for i in range(a + 1, b - 1)]
+            runs += [(b - 1, q, q + 1) for q in range(4)] if last else [(b - 1, 0, 4)]
+            units = [(i, q) for i, lo, hi in runs for q in range(lo, hi)]
             state = [0, 0]
 
             def scalar_ahead(upto):
                 while state[1] < upto and state[0] < len(runs):
-                    i, lo, hi, sq = runs[state[0]]
-                    if sq:
-                        do_qa(i, hi)
+                    i, lo, hi = runs[state[0]]
+                    if i == a + K_ACT and lo == 0 and A_TILES > 0:
+                        do_qa(gb - 1, A_TILES)
                     do_e(i, lo, hi)
                     state[0] = state[0] + 1
                     state[1] = state[1] + hi - lo
                 if state[0] == len(runs) and upto > len(units):
-                    next_g(min(NG, b + PRE_G))
+                    next_g(min(NG, gb + PRE_G))
 
             scalar_ahead(4 * LEAD)
             for u in units[0:4]:
@@ -271,5 +300,9 @@ def tile_longtermattention_t_kernel(tc, theta, basis_mu, basis_sigma, Bv, out):
                 do_p(units[k][0], units[k][1])
                 if k + 4 < len(units):
                     do_et(units[k + 4][0], units[k + 4][1])
-            done[0] = b
+                if k % 4 == 3:
+                    done[0] = units[k][0] + 1
+                    if last and done[0] - a >= TAIL_FROM:
+                        emit_quant(2)
+            ga = gb
         flush()

@@ -24,16 +24,19 @@ FIRST_SB = 8
 OB = 2
 HEAD = 16
 
-A_TILES = 2
+A_TILES = (2, 1, 2)
 K_ACT = 7
 FINE = 0
-POOL_PIECES = 1
+FIRST_CUTS = (1, 2, 3)
 EV_DVE_EVERY = 99
 LEAD = 3
 EV_LAG = 1
-TAIL_FROM = 9
-FL_G = 6
-PRE_G = 2
+TAIL_FROM = 10
+TILEWISE = 1
+HALFWISE = 0
+UNPAIRED = 99
+FL_G = ()
+PRE_G = 3
 
 
 def tile_longtermattention_t_kernel(tc, theta, basis_mu, basis_sigma, Bv, out):
@@ -41,7 +44,7 @@ def tile_longtermattention_t_kernel(tc, theta, basis_mu, basis_sigma, Bv, out):
     with ExitStack() as ctx:
         const = ctx.enter_context(tc.tile_pool(name="const", bufs=1))
         gpool = ctx.enter_context(tc.tile_pool(name="gpool", bufs=BUFS))
-        zpool = ctx.enter_context(tc.tile_pool(name="zpool", bufs=BUFS))
+        zpool = ctx.enter_context(tc.tile_pool(name="zpool", bufs=BUFS // 2))
         qpool = ctx.enter_context(tc.tile_pool(name="qpool", bufs=4))
         spool = ctx.enter_context(tc.tile_pool(name="spool", bufs=3))
         opool = ctx.enter_context(tc.tile_pool(name="opool", bufs=4))
@@ -64,34 +67,35 @@ def tile_longtermattention_t_kernel(tc, theta, basis_mu, basis_sigma, Bv, out):
         parts = []
         for lo, hi, nm in ((0, HEAD, "a"), (HEAD, P, "b")):
             w = hi - lo
-            rec = const.tile([P, w], F32, name="rec" + nm)
             mu = const.tile([P, w], F32, name="mu" + nm)
-            parts.append((lo, hi, rec, mu))
-        sig = const.tile([P, P], F32)
+            parts.append((lo, hi, mu))
+        rec = const.tile([P, P], F32)
 
-        def head_part(k):
-            lo, hi, rec, mu = parts[k]
-            nc.vector.reciprocal(out=rec[:], in_=th[:, lo:hi, 1])
-            nc.vector.tensor_scalar_mul(out=sig[:, lo:hi], in0=rec[:], scalar1=-0.5)
-            nc.vector.tensor_tensor(out=mu[:], in0=sig[:, lo:hi], in1=th[:, lo:hi, 0], op=ALU.mult)
+        def head_part(k, step):
+            lo, hi, mu = parts[k]
+            if step == 0:
+                nc.vector.reciprocal(out=rec[:, lo:hi], in_=th[:, lo:hi, 1])
+            else:
+                nc.vector.scalar_tensor_tensor(out=mu[:], in0=rec[:, lo:hi], scalar=-0.5, in1=th[:, lo:hi, 0],
+                                               op0=ALU.mult, op1=ALU.mult)
 
         def mu_col(c):
-            lo, hi, rec, mu = parts[0 if c < HEAD else 1]
+            lo, hi, mu = parts[0 if c < HEAD else 1]
             return mu[:, c - lo:c - lo + 1]
 
-        sb, gt, gp, zt, ep, rt, ot, osb = {}, {}, {}, {}, {}, {}, {}, {}
+        zz, sb, gt, gp, zt, ep, rt, ot, osb = {}, {}, {}, {}, {}, {}, {}, {}, {}
 
         def do_s(i):
             t = ps_o.tile([P, 512], F32, name="acc")
             for q in range(4):
-                nc.tensor.transpose(t[:, P * q:P * (q + 1)], sig[:, 4 * i + q:4 * i + q + 1].to_broadcast([P, P]), ident[:])
+                nc.tensor.transpose(t[:, P * q:P * (q + 1)], rec[:, 4 * i + q:4 * i + q + 1].to_broadcast([P, P]), ident[:])
             sb[i] = t[:]
 
         def store_sigma():
             t = ps_o.tile([P, 512], F32, name="acc")
-            nc.tensor.transpose(t[:, 0:P], sig[:], ident[:])
+            nc.tensor.transpose(t[:, 0:P], rec[:], ident[:])
             sgt = const.tile([P, P], F32)
-            nc.vector.tensor_copy(out=sgt[:], in_=t[:, 0:P])
+            nc.scalar.copy(out=sgt[:], in_=t[:, 0:P])
             nc.sync.dma_start(out=out[N - P:N, :], in_=sgt[:])
 
         def load_sigma(k):
@@ -101,7 +105,7 @@ def tile_longtermattention_t_kernel(tc, theta, basis_mu, basis_sigma, Bv, out):
             for j in range(2):
                 sb[2 * k + j] = t[:, 512 * j:512 * (j + 1)]
 
-        head_part(0)
+        head_part(0, 0)
         do_s(0)
         do_s(1)
         b2 = const.tile([P, 4], F32)
@@ -109,27 +113,25 @@ def tile_longtermattention_t_kernel(tc, theta, basis_mu, basis_sigma, Bv, out):
                                        op0=ALU.mult, op1=ALU.mult)
         bm = const.tile([P, 4], F32)
         nc.vector.tensor_copy(out=bm[:], in_=bm_raw[:])
+        head_part(0, 1)
         bmp = ps_t.tile([P, 512], F32, name="tp")
         for t in range(4):
             nc.tensor.transpose(bmp[:, P * t:P * (t + 1)], bm[:, t:t + 1].to_broadcast([P, P]), ident[:])
+        bvg = const.tile([P, D, 4], BF16, align_bytes=64)
+        nc.vector.tensor_copy(out=bvg[:], in_=bv_raw[:].rearrange("p t d -> p d t"))
         bmc = const.tile([P, 512], F32)
         nc.vector.tensor_copy(out=bmc[:], in_=bmp[:])
-
-        bvg = const.tile([P, D, 4], BF16, align_bytes=64)
         bvc = const.tile([P, D], U32, align_bytes=64)
         bvs = const.tile([P, D], U8, align_bytes=64)
-
-        def do_bv():
-            nc.vector.tensor_copy(out=bvg[:], in_=bv_raw[:].rearrange("p t d -> p d t"))
-            nc.vector.quantize_mx(out=bvc[:].bitcast(FP8X4), scales=bvs[:],
-                                  in_=bvg[:].rearrange("p d t -> p (d t)"))
+        nc.vector.quantize_mx(out=bvc[:].bitcast(FP8X4), scales=bvs[:],
+                              in_=bvg[:].rearrange("p d t -> p (d t)"))
 
         def do_g(i):
             g = gpool.tile([P, 4, 512], F32, name="g")
-            for cs in [slice(c, c + (128 if i == 0 else 512)) for c in range(0, 512, 128 if i == 0 else 512)]:
+            for cs in (slice(0, 128), slice(128, 512)) if i == 0 else (slice(0, 512),):
                 for t in range(4):
                     nc.scalar.activation(out=g[:, t, cs], in_=sb[i][:, cs], func=ACT.Abs_reciprocal_sqrt,
-                                         bias=b2[:, t:t + 1], scale=TWO_PI)
+                                         bias=b2[:, t:t + 1], scale=-math.pi)
             gt[i] = g
 
         def do_t(i, q):
@@ -139,17 +141,21 @@ def tile_longtermattention_t_kernel(tc, theta, basis_mu, basis_sigma, Bv, out):
             gp[(i, q)] = t_ps
 
         def do_z(i, q):
-            if q == 0:
-                zt[i] = zpool.tile([P, 4, 512], F32, name="z", align_bytes=64)
+            if q == 0 and i % 2 == 0:
+                z = zpool.tile([P, 8, 512], F32, name="z", align_bytes=64)
+                zt[i] = z[:, 0:4, :]
+                zt[i + 1] = z[:, 4:8, :]
+                zz[i] = z
             nc.vector.scalar_tensor_tensor(out=zt[i][:, q, :], in0=bmc[:], scalar=mu_col(4 * i + q),
                                            in1=gp[(i, q)][:], op0=ALU.subtract, op1=ALU.mult)
 
         def sq_view(i, a, b):
             return zt[i][:, a:b, :].rearrange("p q n -> p (q n)")
 
-        def do_qg(i, lo=0, step=4 // POOL_PIECES):
-            for a in range(lo, 4, step):
-                v = sq_view(i, a, min(4, a + step))
+        def do_qg(i, lo=0, cuts=()):
+            edges = [lo] + list(cuts) + [4]
+            for x, y in zip(edges, edges[1:]):
+                v = sq_view(i, x, y)
                 nc.gpsimd.tensor_tensor(out=v, in0=v, in1=v, op=ALU.mult)
 
         def do_qa(i, hi):
@@ -168,7 +174,7 @@ def tile_longtermattention_t_kernel(tc, theta, basis_mu, basis_sigma, Bv, out):
 
         def do_p(i, q):
             if q == 0:
-                rt[i] = zt[i][:].rearrange("p q n -> p (q n)").bitcast(BF16)[:, 0:2048].rearrange(
+                rt[i] = zt[i].rearrange("p q n -> p (q n)").bitcast(BF16)[:, 0:2048].rearrange(
                     "p (n t) -> p n t", t=4)
             cs = slice(P * q, P * (q + 1))
             nc.vector.tensor_tensor(
@@ -209,10 +215,8 @@ def tile_longtermattention_t_kernel(tc, theta, basis_mu, basis_sigma, Bv, out):
         done = [0, 0, 0]
 
         def emit_quant(n, more=False):
-            if done[1] == 0 and done[0] > 0:
-                do_bv()
             for k in range(min(n, done[0] - done[1])):
-                if more and k == FL_G:
+                if more and k in FL_G:
                     next_g(NG)
                 do_quant(done[1])
                 done[1] = done[1] + 1
@@ -247,11 +251,12 @@ def tile_longtermattention_t_kernel(tc, theta, basis_mu, basis_sigma, Bv, out):
             b = a + size
             gb = min(NG, b + LOOK)
             last = b == NG
+            paired = range(ga, gb - UNPAIRED)
             for i in range(ga, gb):
                 next_g(min(gb, i + 2))
                 if i == 0:
                     next_g(min(gb, i + 2))
-                if i == 1:
+                if i == 2:
                     store_sigma()
                     load_sigma(FIRST_SB // 2)
                 if i == ga:
@@ -264,18 +269,24 @@ def tile_longtermattention_t_kernel(tc, theta, basis_mu, basis_sigma, Bv, out):
                     for q in range(4):
                         do_t(i, q)
                         do_z(i, q)
-                if i == 0:
-                    head_part(1)
+                        if i == 1 and q < 2:
+                            head_part(1, q)
                 next_s()
                 next_s()
                 if i == ga:
-                    do_qg(i, 0, 1)
+                    do_qg(i, 0, FIRST_CUTS)
                 elif i < gb - 1:
-                    do_qg(i)
-                elif A_TILES < 4:
-                    do_qg(i, A_TILES, 1)
-            runs = [(a, q, q + 1) for q in range(4)]
-            runs += [(i, 0, 4) for i in range(a + 1, b - 1)]
+                    if (i + (i % 2 == 0)) in paired and i - (i % 2) > ga:
+                        if i % 2 == 1:
+                            v = zz[i - 1][:].rearrange("p q n -> p (q n)")
+                            nc.gpsimd.tensor_tensor(out=v, in0=v, in1=v, op=ALU.mult)
+                    else:
+                        do_qg(i)
+                elif A_TILES[ph] < 4:
+                    do_qg(i, A_TILES[ph], range(A_TILES[ph] + 1, 4))
+            runs = [(i, q, q + 1) for i in range(a, a + TILEWISE) for q in range(4)]
+            runs += [(i, q, q + 2) for i in range(a + TILEWISE, a + TILEWISE + HALFWISE) for q in (0, 2)]
+            runs += [(i, 0, 4) for i in range(a + TILEWISE + HALFWISE, b - 1)]
             runs += [(b - 1, q, q + 1) for q in range(4)] if last else [(b - 1, 0, 4)]
             units = [(i, q) for i, lo, hi in runs for q in range(lo, hi)]
             state = [0, 0]
@@ -283,8 +294,8 @@ def tile_longtermattention_t_kernel(tc, theta, basis_mu, basis_sigma, Bv, out):
             def scalar_ahead(upto):
                 while state[1] < upto and state[0] < len(runs):
                     i, lo, hi = runs[state[0]]
-                    if i == a + K_ACT and lo == 0 and A_TILES > 0:
-                        do_qa(gb - 1, A_TILES)
+                    if i == a + K_ACT and lo == 0 and A_TILES[ph] > 0:
+                        do_qa(gb - 1, A_TILES[ph])
                     do_e(i, lo, hi)
                     state[0] = state[0] + 1
                     state[1] = state[1] + hi - lo

@@ -24,7 +24,7 @@ FIRST_SB = 8
 OB = 2
 HEAD = 16
 
-A_TILES = (2, 1, 2)
+A_TILES = (2, 0, 2)
 K_ACT = 7
 FINE = 0
 FIRST_CUTS = (1, 2, 3)
@@ -34,7 +34,7 @@ EV_LAG = 1
 TAIL_FROM = 10
 TILEWISE = 1
 HALFWISE = 0
-UNPAIRED = 99
+UNPAIRED = 3
 FL_G = ()
 PRE_G = 3
 

from contextlib import ExitStack
import math

import concourse.mybir as mybir
from concourse.masks import make_identity

F32 = mybir.dt.float32
BF16 = mybir.dt.bfloat16
U32 = mybir.dt.uint32
U8 = mybir.dt.uint8
FP8X4 = mybir.dt.float8_e4m3fn_x4
ACT = mybir.ActivationFunctionType
ALU = mybir.AluOpType

N, NB, D = 16384, 512, 128
FLOPS = 2 * N * NB * D
P = 128
NG = 32
SIZES = (10, 10, 12)
BUFS = 12
LOOK = 2
TWO_PI = 2.0 * math.pi
FIRST_SB = 8
OB = 2
HEAD = 16

A_TILES = (2, 0, 2)
K_ACT = 7
FINE = 0
FIRST_CUTS = (1, 2, 3)
EV_DVE_EVERY = 99
LEAD = 3
EV_LAG = 1
TAIL_FROM = 10
TILEWISE = 1
HALFWISE = 0
UNPAIRED = 3
FL_G = ()
PRE_G = 3


def tile_longtermattention_t_kernel(tc, theta, basis_mu, basis_sigma, Bv, out):
    nc = tc.nc
    with ExitStack() as ctx:
        const = ctx.enter_context(tc.tile_pool(name="const", bufs=1))
        gpool = ctx.enter_context(tc.tile_pool(name="gpool", bufs=BUFS))
        zpool = ctx.enter_context(tc.tile_pool(name="zpool", bufs=BUFS // 2))
        qpool = ctx.enter_context(tc.tile_pool(name="qpool", bufs=4))
        spool = ctx.enter_context(tc.tile_pool(name="spool", bufs=3))
        opool = ctx.enter_context(tc.tile_pool(name="opool", bufs=4))
        ps_t = ctx.enter_context(tc.psum_pool(name="ps_t", bufs=4))
        ps_o = ctx.enter_context(tc.psum_pool(name="ps_o", bufs=4))
        ctx.enter_context(tc.manual_schedule())

        th = const.tile([P, P, 2], BF16)
        nc.sync.dma_start(out=th[:], in_=theta.rearrange("(p c) k -> p c k", c=P))
        bs_raw = const.tile([P, 4], BF16)
        nc.sync.dma_start(out=bs_raw[:], in_=basis_sigma.rearrange("(p t) -> p t", t=4))
        bm_raw = const.tile([P, 4], BF16)
        nc.sync.dma_start(out=bm_raw[:], in_=basis_mu.rearrange("(p t) -> p t", t=4))
        bv_raw = const.tile([P, 4, D], BF16)
        nc.sync.dma_start(out=bv_raw[:], in_=Bv.rearrange("(p t) d -> p t d", t=4))

        ident = const.tile([P, P], F32)
        make_identity(nc, ident[:])

        parts = []
        for lo, hi, nm in ((0, HEAD, "a"), (HEAD, P, "b")):
            w = hi - lo
            mu = const.tile([P, w], F32, name="mu" + nm)
            parts.append((lo, hi, mu))
        rec = const.tile([P, P], F32)

        def head_part(k, step):
            lo, hi, mu = parts[k]
            if step == 0:
                nc.vector.reciprocal(out=rec[:, lo:hi], in_=th[:, lo:hi, 1])
            else:
                nc.vector.scalar_tensor_tensor(out=mu[:], in0=rec[:, lo:hi], scalar=-0.5, in1=th[:, lo:hi, 0],
                                               op0=ALU.mult, op1=ALU.mult)

        def mu_col(c):
            lo, hi, mu = parts[0 if c < HEAD else 1]
            return mu[:, c - lo:c - lo + 1]

        zz, sb, gt, gp, zt, ep, rt, ot, osb = {}, {}, {}, {}, {}, {}, {}, {}, {}

        def do_s(i):
            t = ps_o.tile([P, 512], F32, name="acc")
            for q in range(4):
                nc.tensor.transpose(t[:, P * q:P * (q + 1)], rec[:, 4 * i + q:4 * i + q + 1].to_broadcast([P, P]), ident[:])
            sb[i] = t[:]

        def store_sigma():
            t = ps_o.tile([P, 512], F32, name="acc")
            nc.tensor.transpose(t[:, 0:P], rec[:], ident[:])
            sgt = const.tile([P, P], F32)
            nc.scalar.copy(out=sgt[:], in_=t[:, 0:P])
            nc.sync.dma_start(out=out[N - P:N, :], in_=sgt[:])

        def load_sigma(k):
            t = spool.tile([P, 1024], F32, name="sgb")
            lo = N - P + 8 * k
            nc.sync.dma_start(out=t[:], in_=out[lo:lo + 8, :].rearrange("c m -> (c m)").partition_broadcast(P))
            for j in range(2):
                sb[2 * k + j] = t[:, 512 * j:512 * (j + 1)]

        head_part(0, 0)
        do_s(0)
        do_s(1)
        b2 = const.tile([P, 4], F32)
        nc.vector.scalar_tensor_tensor(out=b2[:], in0=bs_raw[:], scalar=TWO_PI, in1=bs_raw[:],
                                       op0=ALU.mult, op1=ALU.mult)
        bm = const.tile([P, 4], F32)
        nc.vector.tensor_copy(out=bm[:], in_=bm_raw[:])
        head_part(0, 1)
        bmp = ps_t.tile([P, 512], F32, name="tp")
        for t in range(4):
            nc.tensor.transpose(bmp[:, P * t:P * (t + 1)], bm[:, t:t + 1].to_broadcast([P, P]), ident[:])
        bvg = const.tile([P, D, 4], BF16, align_bytes=64)
        nc.vector.tensor_copy(out=bvg[:], in_=bv_raw[:].rearrange("p t d -> p d t"))
        bmc = const.tile([P, 512], F32)
        nc.vector.tensor_copy(out=bmc[:], in_=bmp[:])
        bvc = const.tile([P, D], U32, align_bytes=64)
        bvs = const.tile([P, D], U8, align_bytes=64)
        nc.vector.quantize_mx(out=bvc[:].bitcast(FP8X4), scales=bvs[:],
                              in_=bvg[:].rearrange("p d t -> p (d t)"))

        def do_g(i):
            g = gpool.tile([P, 4, 512], F32, name="g")
            for cs in (slice(0, 128), slice(128, 512)) if i == 0 else (slice(0, 512),):
                for t in range(4):
                    nc.scalar.activation(out=g[:, t, cs], in_=sb[i][:, cs], func=ACT.Abs_reciprocal_sqrt,
                                         bias=b2[:, t:t + 1], scale=-math.pi)
            gt[i] = g

        def do_t(i, q):
            t_ps = ps_t.tile([P, 512], F32, name="tp")
            for t in range(4):
                nc.tensor.transpose(t_ps[:, P * t:P * (t + 1)], gt[i][:, t, P * q:P * (q + 1)], ident[:])
            gp[(i, q)] = t_ps

        def do_z(i, q):
            if q == 0 and i % 2 == 0:
                z = zpool.tile([P, 8, 512], F32, name="z", align_bytes=64)
                zt[i] = z[:, 0:4, :]
                zt[i + 1] = z[:, 4:8, :]
                zz[i] = z
            nc.vector.scalar_tensor_tensor(out=zt[i][:, q, :], in0=bmc[:], scalar=mu_col(4 * i + q),
                                           in1=gp[(i, q)][:], op0=ALU.subtract, op1=ALU.mult)

        def sq_view(i, a, b):
            return zt[i][:, a:b, :].rearrange("p q n -> p (q n)")

        def do_qg(i, lo=0, cuts=()):
            edges = [lo] + list(cuts) + [4]
            for x, y in zip(edges, edges[1:]):
                v = sq_view(i, x, y)
                nc.gpsimd.tensor_tensor(out=v, in0=v, in1=v, op=ALU.mult)

        def do_qa(i, hi):
            v = sq_view(i, 0, hi)
            nc.scalar.activation(out=v, in_=v, func=ACT.Square)

        def do_e(i, lo, hi):
            v = sq_view(i, lo, hi)
            nc.scalar.activation(out=v, in_=v, func=ACT.Exp, scale=-math.pi)

        def do_et(i, q):
            t_ps = ps_t.tile([P, 512], F32, name="tp")
            for t in range(4):
                nc.tensor.transpose(t_ps[:, P * t:P * (t + 1)], zt[i][:, q, P * t:P * (t + 1)], ident[:])
            ep[(i, q)] = t_ps

        def do_p(i, q):
            if q == 0:
                rt[i] = zt[i].rearrange("p q n -> p (q n)").bitcast(BF16)[:, 0:2048].rearrange(
                    "p (n t) -> p n t", t=4)
            cs = slice(P * q, P * (q + 1))
            nc.vector.tensor_tensor(
                out=rt[i][:, cs, :].rearrange("p (c i) t -> p c t i", i=4),
                in0=ep[(i, q)][:].rearrange("p (t c i) -> p c t i", t=4, i=4),
                in1=gt[i][:, :, cs].rearrange("p t (c i) -> p c t i", i=4),
                op=ALU.mult)

        def do_quant(i):
            codes = qpool.tile([P, 512], U32, name="codes", align_bytes=64)
            scl = qpool.tile([P, 512], U8, name="scl", align_bytes=64)
            nc.vector.quantize_mx(out=codes[:].bitcast(FP8X4), scales=scl[:],
                                  in_=rt[i].rearrange("p n t -> p (n t)"))
            acc = ps_o.tile([P, 512], F32, name="acc")
            for q in range(4):
                cs = slice(P * q, P * (q + 1))
                nc.tensor.matmul_mx(out=acc[:, cs], lhsT=codes[:, cs].bitcast(FP8X4),
                                    lhsT_scale=scl[:, cs], rhs=bvc[:].bitcast(FP8X4),
                                    rhs_scale=bvs[:], start=True, stop=True)
            ot[i] = acc

        out_v = out.rearrange("(p c) d -> p c d", c=P)

        def do_evac(i):
            s, q = divmod(i, OB)
            if q == 0:
                osb[s] = opool.tile([P, 4 * OB, D], F32, name="osb")
            dst = osb[s][:, 4 * q:4 * q + 4, :].rearrange("p c d -> p (c d)")
            if i % EV_DVE_EVERY == EV_DVE_EVERY - 1:
                nc.vector.tensor_copy(out=dst, in_=ot[i][:])
            else:
                nc.scalar.copy(out=dst, in_=ot[i][:])
            if s == NG // OB - 1:
                nc.sync.dma_start(out=out_v[:, 4 * i:4 * i + 4, :], in_=osb[s][:, 4 * q:4 * q + 4, :])
            elif q == OB - 1:
                nc.sync.dma_start(out=out_v[:, 4 * OB * s:4 * OB * (s + 1), :], in_=osb[s][:])

        done = [0, 0, 0]

        def emit_quant(n, more=False):
            for k in range(min(n, done[0] - done[1])):
                if more and k in FL_G:
                    next_g(NG)
                do_quant(done[1])
                done[1] = done[1] + 1
                if done[1] - done[2] > EV_LAG:
                    do_evac(done[2])
                    done[2] = done[2] + 1

        def flush(more=False):
            emit_quant(NG, more)
            for i in range(done[2], done[1]):
                do_evac(i)
            done[2] = done[1]

        made = [0]
        spread = [2]

        def next_g(limit):
            if made[0] < limit:
                do_g(made[0])
                made[0] = made[0] + 1
                if made[0] % 2 == 0 and FIRST_SB < made[0] + 4 < NG:
                    load_sigma(made[0] // 2 + 2)

        def next_s():
            if spread[0] < min(FIRST_SB, made[0] + 2):
                do_s(spread[0])
                spread[0] = spread[0] + 1

        ga = 0
        for ph, size in enumerate(SIZES):
            a = sum(SIZES[:ph])
            b = a + size
            gb = min(NG, b + LOOK)
            last = b == NG
            paired = range(ga, gb - UNPAIRED)
            for i in range(ga, gb):
                next_g(min(gb, i + 2))
                if i == 0:
                    next_g(min(gb, i + 2))
                if i == 2:
                    store_sigma()
                    load_sigma(FIRST_SB // 2)
                if i == ga:
                    for q in range(4):
                        do_t(i, q)
                    flush(i > 0)
                    for q in range(4):
                        do_z(i, q)
                else:
                    for q in range(4):
                        do_t(i, q)
                        do_z(i, q)
                        if i == 1 and q < 2:
                            head_part(1, q)
                next_s()
                next_s()
                if i == ga:
                    do_qg(i, 0, FIRST_CUTS)
                elif i < gb - 1:
                    if (i + (i % 2 == 0)) in paired and i - (i % 2) > ga:
                        if i % 2 == 1:
                            v = zz[i - 1][:].rearrange("p q n -> p (q n)")
                            nc.gpsimd.tensor_tensor(out=v, in0=v, in1=v, op=ALU.mult)
                    else:
                        do_qg(i)
                elif A_TILES[ph] < 4:
                    do_qg(i, A_TILES[ph], range(A_TILES[ph] + 1, 4))
            runs = [(i, q, q + 1) for i in range(a, a + TILEWISE) for q in range(4)]
            runs += [(i, q, q + 2) for i in range(a + TILEWISE, a + TILEWISE + HALFWISE) for q in (0, 2)]
            runs += [(i, 0, 4) for i in range(a + TILEWISE + HALFWISE, b - 1)]
            runs += [(b - 1, q, q + 1) for q in range(4)] if last else [(b - 1, 0, 4)]
            units = [(i, q) for i, lo, hi in runs for q in range(lo, hi)]
            state = [0, 0]

            def scalar_ahead(upto):
                while state[1] < upto and state[0] < len(runs):
                    i, lo, hi = runs[state[0]]
                    if i == a + K_ACT and lo == 0 and A_TILES[ph] > 0:
                        do_qa(gb - 1, A_TILES[ph])
                    do_e(i, lo, hi)
                    state[0] = state[0] + 1
                    state[1] = state[1] + hi - lo
                if state[0] == len(runs) and upto > len(units):
                    next_g(min(NG, gb + PRE_G))

            scalar_ahead(4 * LEAD)
            for u in units[0:4]:
                do_et(u[0], u[1])
            for k in range(len(units)):
                if k % 4 == 0:
                    scalar_ahead(k + 4 + 4 * LEAD)
                do_p(units[k][0], units[k][1])
                if k + 4 < len(units):
                    do_et(units[k + 4][0], units[k + 4][1])
                if k % 4 == 3:
                    done[0] = units[k][0] + 1
                    if last and done[0] - a >= TAIL_FROM:
                        emit_quant(2)
            ga = gb
        flush()
